import numpy as np
import ml_dtypes


def mxq(x, axis, fmt="e4m3"):
    dtype, down = {"e4m3": (ml_dtypes.float8_e4m3fn, 7), "e5m2": (ml_dtypes.float8_e5m2, 14)}[fmt]
    v = np.moveaxis(np.asarray(x, np.float32).astype(ml_dtypes.bfloat16).astype(np.float64), axis, -1)
    blocks = v.reshape(v.shape[:-1] + (-1, 32))
    amax = np.abs(blocks).max(-1, keepdims=True)
    byte = np.maximum(np.where(amax > 0, np.frexp(amax)[1] - 1 + 127, 0) - down, 1)
    scale = np.exp2(byte - 127.0)
    codes = (blocks / scale).astype(np.float32).astype(dtype).astype(np.float64)
    return np.moveaxis((codes * scale).reshape(v.shape), -1, axis)


WIDE = False


def mx_kscale(k):
    if not WIDE:
        return np.ones(k)
    levels = np.array([18, -18])
    if k % 512:
        return np.exp2(np.random.permutation(np.resize(levels, k // 32))).repeat(32)
    a = np.empty((k // 512, 16))
    for p in range(k // 512):
        a[p, :8] = np.random.permutation(np.resize(levels, 8))
        for g in range(8):
            far = levels[np.abs(levels - a[p, g]) >= 10]
            a[p, g + 8] = far[np.random.randint(len(far))]
    return np.exp2(a.ravel()).repeat(32)


BF16 = ml_dtypes.bfloat16


def bf(x):
    return np.asarray(x, np.float32).astype(BF16)


def f64(x):
    return np.asarray(x).astype(np.float64)


B, N, D = 4, 256, 512
BN = B * N
DM = D + D


def sigmoid(v):
    return 1.0 / (1.0 + np.exp(-v))


def setup_inputs():
    s = mx_kscale(BN).reshape(B, N, 1)
    u = mx_kscale(D)
    node_state = bf(np.random.standard_normal((B, N, D)))
    m0 = bf(np.random.standard_normal((B, N, DM)))
    h_tilda = bf(np.tanh(np.random.standard_normal((BN, D))))
    mask = bf(np.random.uniform(size=(B, N)) < 0.9)
    w0 = bf(np.random.standard_normal((DM, D)) / np.sqrt(DM))
    u_z = bf(np.random.standard_normal((D, D)) / np.sqrt(D))
    g = bf(np.random.standard_normal((B, N, D)) * np.exp2(np.random.randint(-6, 1, (B, N, 1))) * 8.0 / s * u)
    z_t = sigmoid(f64(m0).reshape(BN, DM) @ f64(w0) + f64(node_state).reshape(BN, D) @ f64(u_z))
    return {"node_state": node_state,
            "message": bf(f64(m0) * s),
            "h_tilda": h_tilda,
            "mask": mask,
            "w_z": bf(f64(w0) / u),
            "u_z": u_z,
            "z_t": np.asarray(z_t, np.float32),
            "grad_out": g}


def reference(node_state, message, h_tilda, mask, w_z, u_z, z_t, grad_out):
    h = f64(node_state).reshape(BN, D)
    m = f64(message).reshape(BN, DM)
    z = f64(z_t)
    g = f64(grad_out).reshape(BN, D) * f64(mask).reshape(BN)[:, None]
    da = g * (f64(h_tilda) - h) * (z * (1.0 - z))
    dm = mxq(da, 1, "e5m2") @ mxq(f64(w_z), 1, "e4m3").T
    dw = mxq(m, 0, "e4m3").T @ mxq(da, 0, "e5m2")
    return dm.reshape(B, N, DM), dw

@@ -1,0 +1,388 @@
+from contextlib import ExitStack
+
+import concourse.mybir as mybir
+from concourse.masks import make_identity
+
+TOKENS, FEATS, MSG = 1024, 512, 1024
+FLOPS = 2 * 2 * TOKENS * FEATS * MSG
+BYTES = 2 * TOKENS * (3 * FEATS + MSG + 1) + 2 * MSG * FEATS + 4 * TOKENS * FEATS + 4 * (TOKENS * MSG + MSG * FEATS)
+
+F32 = mybir.dt.float32
+BF16 = mybir.dt.bfloat16
+U32 = mybir.dt.uint32
+U8 = mybir.dt.uint8
+E4M3 = mybir.dt.float8_e4m3fn_x4
+E5M2 = mybir.dt.float8_e5m2_x4
+ADD = mybir.AluOpType.add
+MULT = mybir.AluOpType.mult
+
+P = 128
+PASSES = 2
+SLOTS = 4
+PAIRS = 4
+
+
+def tile_updatefunction_pb_v_kernel(
+    tc, node_state, message, h_tilda, mask, w_z, u_z, z_t, grad_out, out_0, out_1
+):
+    nc = tc.nc
+    by_slot = "(g p j) w -> g p j w"
+    hv = node_state.rearrange("b n w -> (b n) w").rearrange(by_slot, g=PASSES, j=SLOTS)
+    tv = h_tilda.rearrange(by_slot, g=PASSES, j=SLOTS)
+    zv = z_t.rearrange(by_slot, g=PASSES, j=SLOTS)
+    gv = grad_out.rearrange("b n w -> (b n) w").rearrange(by_slot, g=PASSES, j=SLOTS)
+    mv = message.rearrange("b n w -> (b n) w").rearrange(by_slot, g=PASSES, j=SLOTS)
+    kv = mask.rearrange("b n -> (b n)").rearrange("(g p j) -> p g j", g=PASSES, j=SLOTS)
+    wv = w_z.rearrange("(i p r) d -> i p r d", i=2, r=4)
+    o0v = out_0.rearrange("b n w -> (b n) w").rearrange(by_slot, g=PASSES, j=SLOTS)
+    o1v = out_1.rearrange("(m p) d -> p m d", p=P)
+
+    with ExitStack() as ctx:
+        keep = ctx.enter_context(tc.tile_pool(name="keep", bufs=1))
+        work = ctx.enter_context(tc.tile_pool(name="work", bufs=3))
+        psum = ctx.enter_context(tc.psum_pool(name="psum", bufs=2))
+
+        def kept(name, shape, dtype):
+            return keep.tile(shape, dtype, name=name, align_bytes=64)
+
+        ident = kept("ident", [P, P], F32)
+        plus = kept("plus", [P, P], BF16)
+        minus = kept("minus", [P, P], BF16)
+        mk = kept("mk", [P, PASSES, SLOTS], BF16)
+        z = [kept(f"z{c}", [P, 2, FEATS], F32) for c in range(PAIRS)]
+        h = [kept(f"h{c}", [P, 2, FEATS], BF16) for c in range(PAIRS)]
+        t = [kept(f"t{c}", [P, 2, FEATS], BF16) for c in range(PAIRS)]
+        g = [kept(f"g{c}", [P, 2, FEATS], BF16) for c in range(PAIRS)]
+        w_raw = [kept(f"w_raw{i}", [P, 4, FEATS], BF16) for i in range(2)]
+        m_raw = [kept(f"m_raw{k}", [P, SLOTS, MSG], BF16) for k in range(PASSES)]
+
+        da = [kept(f"da{k}", [P, SLOTS, FEATS], BF16) for k in range(PASSES)]
+        da_tok = [kept(f"da_tok{k}", [P, FEATS, 4], BF16) for k in range(PASSES)]
+        da_feat = [kept(f"da_feat{c}", [P, 2 * P * 4], BF16) for c in range(PAIRS)]
+        m_tok = [kept(f"m_tok{k}", [P, MSG, 4], BF16) for k in range(PASSES)]
+        w_feat = [kept(f"w_feat{i}", [P, 512 * 4], BF16) for i in range(2)]
+
+        def quantised(name, width):
+            return kept(name + "_codes", [P, width], U32), kept(name + "_scales", [P, width], U8)
+
+        q_da_tok = [quantised(f"q_da_tok{k}", FEATS) for k in range(PASSES)]
+        q_da_feat = [quantised(f"q_da_feat{c}", 2 * P) for c in range(PAIRS)]
+        q_m = [quantised(f"q_m{k}", MSG) for k in range(PASSES)]
+        q_w = [quantised(f"q_w{i}", 512) for i in range(2)]
+
+        o0 = [kept(f"o0_{c}", [P, 2, MSG], F32) for c in range(PAIRS)]
+        o1 = kept("o1", [P, 8, FEATS], F32)
+
+        def span(first, count):
+            return first // SLOTS, slice(first % SLOTS, first % SLOTS + count)
+
+        def load(dst, view, first, count):
+            k, slots = span(first, count)
+            own = slice(first % 2, first % 2 + count)
+            nc.sync.dma_start(out=dst[first // 2][:, own, :], in_=view[k][:, slots, :])
+
+        def load_m(k, half):
+            cols = slice(512 * half, 512 * half + 512)
+            nc.sync.dma_start(out=m_raw[k][:, :, cols], in_=mv[k][:, :, cols])
+
+        def load_w(i):
+            nc.sync.dma_start(out=w_raw[i][:], in_=wv[i])
+
+        gates = {}
+        diffs = {}
+        prods = {}
+
+        def gate(s):
+            c, e = s // 2, s % 2
+            gates[s] = work.tile([P, FEATS], F32, name="gate")
+            nc.vector.scalar_tensor_tensor(
+                out=gates[s][:], in0=z[c][:, e, :], scalar=-1.0, in1=z[c][:, e, :], op0=ADD, op1=MULT
+            )
+
+        def diff_vector(s):
+            c, e = s // 2, s % 2
+            diff = work.tile([P, FEATS], F32, name="diff")
+            nc.vector.tensor_sub(out=diff[:], in0=h[c][:, e, :], in1=t[c][:, e, :])
+            diffs[s] = diff
+
+        def diff_tensor(c):
+            pair = [psum.tile([P, FEATS], F32, name="dps") for e in range(2)]
+            for e in range(2):
+                nc.tensor.matmul(pair[e][:], lhsT=plus[:], rhs=h[c][:, e, :], start=True, stop=False)
+            for e in range(2):
+                nc.tensor.matmul(pair[e][:], lhsT=minus[:], rhs=t[c][:, e, :], start=False, stop=True)
+                diffs[2 * c + e] = pair[e]
+
+        def product(s):
+            c, e = s // 2, s % 2
+            prods[s] = work.tile([P, FEATS], F32, name="prod")
+            nc.vector.scalar_tensor_tensor(
+                out=prods[s][:], in0=g[c][:, e, :], scalar=mk[:, s // SLOTS, s % SLOTS : s % SLOTS + 1],
+                in1=diffs[s][:], op0=MULT, op1=MULT,
+            )
+
+        def finish(s):
+            nc.vector.tensor_mul(out=da[s // SLOTS][:, s % SLOTS, :], in0=prods[s][:], in1=gates[s][:])
+
+        def turn_da(c):
+            bank = psum.tile([P, 2, 2, P], F32, name="tps")
+            for e in range(2):
+                words = da[c // 2][:, 2 * (c % 2) + e, :].bitcast(F32)
+                for u in range(2):
+                    nc.tensor.transpose(bank[:, e, u, :], words[:, u : FEATS // 2 : 2], ident[:])
+            diffs["da", c] = bank
+
+        def spread_da(c, copy):
+            copy(
+                out=da_feat[c][:].bitcast(F32).rearrange("p (e k u) -> p e k u", e=2, u=2),
+                in_=diffs["da", c][:].rearrange("p e u k -> p e k u"),
+            )
+
+        def turn_w(i, q):
+            bank = psum.tile([P, 2, 2, P], F32, name="tps")
+            for r in range(2):
+                words = w_raw[i][:, 2 * q + r, :].bitcast(F32)
+                for u in range(2):
+                    nc.tensor.transpose(bank[:, r, u, :], words[:, u : FEATS // 2 : 2], ident[:])
+            diffs["w", i, q] = bank
+
+        def spread_w(i, q, copy):
+            words = w_feat[i][:].bitcast(F32).rearrange("p (k r u) -> p k r u", r=4, u=2)
+            copy(out=words[:, :, 2 * q : 2 * q + 2, :], in_=diffs["w", i, q][:].rearrange("p r u k -> p k r u"))
+
+        def interleave(dst, src, first, width, copy):
+            cols = slice(first, first + width)
+            copy(
+                out=dst[:, cols, :].rearrange("p (c i) t -> p c t i", i=4),
+                in_=src[:, :, cols].rearrange("p t (c i) -> p c t i", i=4),
+            )
+
+        def quantise(dst, src, first, width, fmt):
+            codes, scales = dst
+            nc.vector.quantize_mx(
+                out=codes[:, first : first + width].bitcast(fmt), scales=scales[:, first : first + width], in_=src
+            )
+
+        def q_tok(k, first, width):
+            quantise(q_da_tok[k], da_tok[k][:, first : first + width, :].rearrange("p w t -> p (w t)"), first, width, E5M2)
+
+        def q_feat(c):
+            quantise(q_da_feat[c], da_feat[c][:], 0, 2 * P, E5M2)
+
+        def q_msg(k, first, width):
+            quantise(q_m[k], m_tok[k][:, first : first + width, :].rearrange("p w t -> p (w t)"), first, width, E4M3)
+
+        def q_weight(i):
+            quantise(q_w[i], w_feat[i][:], 0, 512, E4M3)
+
+        banks = {}
+
+        def mx0(s, n):
+            c, e = s // 2, s % 2
+            bank = psum.tile([P, 512], F32, name="mps", bufs=4)
+            cols = slice(P * e, P * e + P)
+            nc.tensor.matmul_mx(
+                out=bank[:], lhsT=q_da_feat[c][0][:, cols].bitcast(E5M2), lhsT_scale=q_da_feat[c][1][:, cols],
+                rhs=q_w[n][0][:].bitcast(E4M3), rhs_scale=q_w[n][1][:], start=True, stop=True,
+            )
+            banks[s, n] = bank
+
+        def out0(s, n, copy):
+            copy(out=o0[s // 2][:, s % 2, 512 * n : 512 * n + 512], in_=banks[s, n][:])
+
+        def store0(c):
+            nc.sync.dma_start(out=o0v[c // 2][:, 2 * (c % 2) : 2 * (c % 2) + 2, :], in_=o0[c][:])
+
+        def store0_slot(s):
+            nc.sync.dma_start(out=o0v[s // 4][:, s % 4, :], in_=o0[s // 2][:, s % 2, :])
+
+        def mx1(m, k, where=None):
+            if k == 0:
+                banks["o1", m] = psum.tile([P, 512], F32, name=where, bufs=4 if where == "mps" else 2)
+            cols = slice(P * m, P * m + P)
+            nc.tensor.matmul_mx(
+                out=banks["o1", m][:], lhsT=q_m[k][0][:, cols].bitcast(E4M3), lhsT_scale=q_m[k][1][:, cols],
+                rhs=q_da_tok[k][0][:].bitcast(E5M2), rhs_scale=q_da_tok[k][1][:], start=(k == 0), stop=(k == 1),
+            )
+
+        def out1(m, copy):
+            copy(out=o1[:, m, :], in_=banks["o1", m][:])
+
+        def store1(m, count):
+            nc.sync.dma_start(out=o1v[:, m : m + count, :], in_=o1[:, m : m + count, :])
+
+        V, S = nc.vector.tensor_copy, nc.scalar.copy
+
+        make_identity(nc, plus[:])
+        nc.gpsimd.memset(minus[:], 0.0)
+        nc.gpsimd.affine_select(
+            out=minus[:], in_=minus[:], compare_op=mybir.AluOpType.not_equal, fill=-1.0, base=0,
+            pattern=[[-1, P]], channel_multiplier=1,
+        )
+        make_identity(nc, ident[:])
+
+        with tc.manual_schedule():
+            load(z, zv, 2, 2)
+            load(h, hv, 2, 2)
+            load(t, tv, 2, 2)
+            load(g, gv, 2, 2)
+            gate(2)
+            nc.sync.dma_start(out=mk[:], in_=kv)
+            load_w(0)
+            diff_tensor(1)
+            load(h, hv, 1, 1)
+            gate(3)
+            turn_w(0, 1)
+            product(2)
+            turn_w(0, 0)
+            load(t, tv, 1, 1)
+            load(t, tv, 0, 1)
+            product(3)
+            load(h, hv, 0, 1)
+            finish(3)
+            load(g, gv, 0, 1)
+            spread_w(0, 1, S)
+            finish(2)
+            turn_da(1)
+            diff_vector(1)
+            load_m(0, 0)
+            diff_vector(0)
+            spread_w(0, 0, S)
+            q_weight(0)
+            spread_da(1, S)
+            load(g, gv, 1, 1)
+            interleave(m_tok[0], m_raw[0], 0, 256, S)
+            product(0)
+            q_feat(1)
+            product(1)
+            mx0(3, 0)
+            load(z, zv, 1, 1)
+            mx0(2, 0)
+            load(z, zv, 0, 1)
+            load_w(1)
+            turn_w(1, 0)
+            interleave(m_tok[0], m_raw[0], 256, 256, S)
+            load(z, zv, 4, 2)
+            load(h, hv, 4, 2)
+            out0(3, 0, S)
+            out0(2, 0, S)
+            load(t, tv, 4, 2)
+            load(g, gv, 4, 2)
+            gate(1)
+            gate(0)
+            load(t, tv, 6, 2)
+            spread_w(1, 0, S)
+            load(h, hv, 6, 2)
+            finish(1)
+            q_msg(0, 0, 512)
+            turn_w(1, 1)
+            diff_tensor(2)
+            spread_w(1, 1, S)
+            finish(0)
+            gate(4)
+            interleave(da_tok[0], da[0], 256, 256, S)
+            load(z, zv, 6, 2)
+            interleave(da_tok[0], da[0], 0, 256, S)
+            gate(5)
+            q_weight(1)
+            mx0(2, 1)
+            turn_da(0)
+            product(4)
+            spread_da(0, S)
+            product(5)
+            finish(4)
+            finish(5)
+            mx0(3, 1)
+            load(g, gv, 6, 2)
+            load_m(1, 0)
+            q_feat(0)
+            out0(2, 1, S)
+            q_tok(0, 0, 512)
+            out0(3, 1, S)
+            diff_tensor(3)
+            mx0(1, 0)
+            load_m(0, 1)
+            gate(7)
+            product(6)
+            out0(1, 0, S)
+            gate(6)
+            product(7)
+            mx0(1, 1)
+            out0(1, 1, S)
+            finish(6)
+            store0_slot(2)
+            turn_da(2)
+            finish(7)
+            store0_slot(3)
+            spread_da(2, S)
+            mx0(0, 0)
+            q_feat(2)
+            mx0(0, 1)
+            interleave(da_tok[1], da[1], 256, 256, V)
+            turn_da(3)
+            mx0(5, 1)
+            out0(0, 0, S)
+            mx1(2, 0, "tps")
+            out0(0, 1, S)
+            interleave(m_tok[1], m_raw[1], 0, 256, S)
+            interleave(da_tok[1], da[1], 0, 256, V)
+            spread_da(3, S)
+            interleave(m_tok[1], m_raw[1], 256, 256, V)
+            store0_slot(1)
+            q_feat(3)
+            out0(5, 1, S)
+            mx0(5, 0)
+            mx0(4, 0)
+            q_tok(1, 0, 512)
+            mx0(4, 1)
+            interleave(m_tok[0], m_raw[0], 512, 256, V)
+            out0(5, 0, S)
+            out0(4, 0, S)
+            out0(4, 1, S)
+            mx0(7, 0)
+            mx1(1, 0, "dps")
+            mx0(7, 1)
+            store0_slot(0)
+            q_msg(1, 0, 512)
+            mx0(6, 1)
+            mx0(6, 0)
+            mx1(2, 1)
+            interleave(m_tok[0], m_raw[0], 768, 256, V)
+            mx1(3, 0, "tps")
+            out0(7, 0, S)
+            out0(7, 1, S)
+            load_m(1, 1)
+            out0(6, 1, S)
+            store0_slot(5)
+            mx1(0, 0, "dps")
+            interleave(m_tok[1], m_raw[1], 768, 256, V)
+            out0(6, 0, S)
+            store0_slot(4)
+            mx1(3, 1)
+            interleave(m_tok[1], m_raw[1], 512, 256, V)
+            q_msg(0, 512, 512)
+            q_msg(1, 512, 512)
+            mx1(0, 1)
+            mx1(1, 1)
+            mx1(5, 0, "mps")
+            mx1(4, 0, "mps")
+            mx1(5, 1)
+            out1(2, S)
+            mx1(4, 1)
+            mx1(7, 0, "mps")
+            out1(3, S)
+            out1(0, S)
+            store0_slot(7)
+            out1(4, V)
+            mx1(7, 1)
+            mx1(6, 0, "mps")
+            out1(1, S)
+            out1(7, V)
+            out1(5, S)
+            store0_slot(6)
+            mx1(6, 1)
+            out1(6, V)
+            store1(2, 2)
+            store1(0, 2)
+            store1(4, 2)
+            store1(6, 2)

@@ -49,10 +49,10 @@ def tile_updatefunction_pb_v_kernel(
         plus = kept("plus", [P, P], BF16)
         minus = kept("minus", [P, P], BF16)
         mk = kept("mk", [P, PASSES, SLOTS], BF16)
-        z = [kept(f"z{c}", [P, 2, FEATS], F32) for c in range(PAIRS)]
-        h = [kept(f"h{c}", [P, 2, FEATS], BF16) for c in range(PAIRS)]
-        t = [kept(f"t{c}", [P, 2, FEATS], BF16) for c in range(PAIRS)]
-        g = [kept(f"g{c}", [P, 2, FEATS], BF16) for c in range(PAIRS)]
+        z = [kept(f"z{k}", [P, SLOTS, FEATS], F32) for k in range(PASSES)]
+        h = [kept(f"h{k}", [P, SLOTS, FEATS], BF16) for k in range(PASSES)]
+        t = [kept(f"t{k}", [P, SLOTS, FEATS], BF16) for k in range(PASSES)]
+        g = [kept(f"g{k}", [P, SLOTS, FEATS], BF16) for k in range(PASSES)]
         w_raw = [kept(f"w_raw{i}", [P, 4, FEATS], BF16) for i in range(2)]
         m_raw = [kept(f"m_raw{k}", [P, SLOTS, MSG], BF16) for k in range(PASSES)]
 
@@ -78,51 +78,59 @@ def tile_updatefunction_pb_v_kernel(
 
         def load(dst, view, first, count):
             k, slots = span(first, count)
-            own = slice(first % 2, first % 2 + count)
-            nc.sync.dma_start(out=dst[first // 2][:, own, :], in_=view[k][:, slots, :])
+            nc.sync.dma_start(out=dst[k][:, slots, :], in_=view[k][:, slots, :])
 
         def load_m(k, half):
             cols = slice(512 * half, 512 * half + 512)
             nc.sync.dma_start(out=m_raw[k][:, :, cols], in_=mv[k][:, :, cols])
 
+        def load_mfull(k):
+            nc.sync.dma_start(out=m_raw[k][:], in_=mv[k])
+
+        def load_mask():
+            nc.sync.dma_start(out=mk[:], in_=kv)
+
         def load_w(i):
             nc.sync.dma_start(out=w_raw[i][:], in_=wv[i])
+
+        def slot(tiles, s):
+            return tiles[s // SLOTS][:, s % SLOTS, :]
+
+        def pair(tiles, c):
+            return tiles[c // 2][:, 2 * (c % 2) : 2 * (c % 2) + 2, :]
 
         gates = {}
         diffs = {}
         prods = {}
 
-        def gate(s):
-            c, e = s // 2, s % 2
-            gates[s] = work.tile([P, FEATS], F32, name="gate")
-            nc.vector.scalar_tensor_tensor(
-                out=gates[s][:], in0=z[c][:, e, :], scalar=-1.0, in1=z[c][:, e, :], op0=ADD, op1=MULT
-            )
+        def gate(c):
+            gates[c] = work.tile([P, 2, FEATS], F32, name="gate")
+            prods[c] = work.tile([P, 2, FEATS], F32, name="prod")
+            nc.vector.scalar_tensor_tensor(out=gates[c][:], in0=pair(z, c), scalar=-1.0, in1=pair(z, c), op0=ADD, op1=MULT)
 
-        def diff_vector(s):
-            c, e = s // 2, s % 2
-            diff = work.tile([P, FEATS], F32, name="diff")
-            nc.vector.tensor_sub(out=diff[:], in0=h[c][:, e, :], in1=t[c][:, e, :])
-            diffs[s] = diff
+        def diff_vector(c):
+            diff = work.tile([P, 2, FEATS], F32, name="diff", bufs=1)
+            nc.vector.tensor_sub(out=diff[:], in0=pair(h, c), in1=pair(t, c))
+            for e in range(2):
+                diffs[2 * c + e] = diff[:, e, :]
 
         def diff_tensor(c):
-            pair = [psum.tile([P, FEATS], F32, name="dps") for e in range(2)]
+            banks2 = [psum.tile([P, FEATS], F32, name="dps") for e in range(2)]
             for e in range(2):
-                nc.tensor.matmul(pair[e][:], lhsT=plus[:], rhs=h[c][:, e, :], start=True, stop=False)
+                nc.tensor.matmul(banks2[e][:], lhsT=plus[:], rhs=slot(h, 2 * c + e), start=True, stop=False)
             for e in range(2):
-                nc.tensor.matmul(pair[e][:], lhsT=minus[:], rhs=t[c][:, e, :], start=False, stop=True)
-                diffs[2 * c + e] = pair[e]
+                nc.tensor.matmul(banks2[e][:], lhsT=minus[:], rhs=slot(t, 2 * c + e), start=False, stop=True)
+                diffs[2 * c + e] = banks2[e][:]
 
         def product(s):
             c, e = s // 2, s % 2
-            prods[s] = work.tile([P, FEATS], F32, name="prod")
             nc.vector.scalar_tensor_tensor(
-                out=prods[s][:], in0=g[c][:, e, :], scalar=mk[:, s // SLOTS, s % SLOTS : s % SLOTS + 1],
-                in1=diffs[s][:], op0=MULT, op1=MULT,
+                out=prods[c][:, e, :], in0=slot(g, s), scalar=mk[:, s // SLOTS, s % SLOTS : s % SLOTS + 1],
+                in1=diffs[s], op0=MULT, op1=MULT,
             )
 
-        def finish(s):
-            nc.vector.tensor_mul(out=da[s // SLOTS][:, s % SLOTS, :], in0=prods[s][:], in1=gates[s][:])
+        def finish(c):
+            nc.vector.tensor_mul(out=pair(da, c), in0=prods[c][:], in1=gates[c][:])
 
         def turn_da(c):
             bank = psum.tile([P, 2, 2, P], F32, name="tps")
@@ -222,167 +230,151 @@ def tile_updatefunction_pb_v_kernel(
         make_identity(nc, ident[:])
 
         with tc.manual_schedule():
-            load(z, zv, 2, 2)
-            load(h, hv, 2, 2)
-            load(t, tv, 2, 2)
-            load(g, gv, 2, 2)
-            gate(2)
-            nc.sync.dma_start(out=mk[:], in_=kv)
-            load_w(0)
-            diff_tensor(1)
-            load(h, hv, 1, 1)
-            gate(3)
-            turn_w(0, 1)
-            product(2)
-            turn_w(0, 0)
-            load(t, tv, 1, 1)
-            load(t, tv, 0, 1)
-            product(3)
-            load(h, hv, 0, 1)
-            finish(3)
-            load(g, gv, 0, 1)
-            spread_w(0, 1, S)
-            finish(2)
-            turn_da(1)
-            diff_vector(1)
-            load_m(0, 0)
+            load(t, tv, 0, 2)
+            load(h, hv, 0, 2)
             diff_vector(0)
-            spread_w(0, 0, S)
-            q_weight(0)
-            spread_da(1, S)
-            load(g, gv, 1, 1)
-            interleave(m_tok[0], m_raw[0], 0, 256, S)
-            product(0)
-            q_feat(1)
-            product(1)
-            mx0(3, 0)
-            load(z, zv, 1, 1)
-            mx0(2, 0)
-            load(z, zv, 0, 1)
-            load_w(1)
-            turn_w(1, 0)
-            interleave(m_tok[0], m_raw[0], 256, 256, S)
-            load(z, zv, 4, 2)
-            load(h, hv, 4, 2)
-            out0(3, 0, S)
-            out0(2, 0, S)
-            load(t, tv, 4, 2)
-            load(g, gv, 4, 2)
-            gate(1)
+            load(z, zv, 0, 2)
             gate(0)
-            load(t, tv, 6, 2)
-            spread_w(1, 0, S)
-            load(h, hv, 6, 2)
-            finish(1)
-            q_msg(0, 0, 512)
-            turn_w(1, 1)
-            diff_tensor(2)
-            spread_w(1, 1, S)
+            load_w(0)
+            load_mask()
+            turn_w(0, 0)
+            load(g, gv, 0, 2)
+            load(h, hv, 2, 2)
+            product(1)
+            product(0)
+            turn_w(0, 1)
             finish(0)
-            gate(4)
-            interleave(da_tok[0], da[0], 256, 256, S)
-            load(z, zv, 6, 2)
-            interleave(da_tok[0], da[0], 0, 256, S)
-            gate(5)
-            q_weight(1)
-            mx0(2, 1)
+            load(t, tv, 2, 2)
+            diff_tensor(1)
+            load(z, zv, 2, 2)
+            load_w(1)
+            spread_w(0, 1, S)
+            gate(1)
+            load(g, gv, 2, 2)
+            spread_w(0, 0, S)
             turn_da(0)
-            product(4)
+            q_weight(0)
             spread_da(0, S)
-            product(5)
-            finish(4)
-            finish(5)
-            mx0(3, 1)
-            load(g, gv, 6, 2)
-            load_m(1, 0)
+            load(z, zv, 4, 2)
+            product(2)
+            product(3)
+            turn_w(1, 0)
+            spread_w(1, 0, S)
+            turn_w(1, 1)
+            spread_w(1, 1, S)
+            load(h, hv, 4, 4)
             q_feat(0)
-            out0(2, 1, S)
-            q_tok(0, 0, 512)
-            out0(3, 1, S)
-            diff_tensor(3)
             mx0(1, 0)
-            load_m(0, 1)
-            gate(7)
-            product(6)
             out0(1, 0, S)
-            gate(6)
-            product(7)
+            finish(1)
+            interleave(da_tok[0], da[0], 256, 256, S)
+            gate(2)
+            load(t, tv, 4, 4)
+            q_weight(1)
+            interleave(da_tok[0], da[0], 0, 256, S)
+            diff_tensor(2)
+            turn_da(1)
             mx0(1, 1)
             out0(1, 1, S)
-            finish(6)
-            store0_slot(2)
-            turn_da(2)
-            finish(7)
-            store0_slot(3)
-            spread_da(2, S)
-            mx0(0, 0)
-            q_feat(2)
+            load(g, gv, 4, 4)
+            product(4)
             mx0(0, 1)
-            interleave(da_tok[1], da[1], 256, 256, V)
-            turn_da(3)
-            mx0(5, 1)
-            out0(0, 0, S)
-            mx1(2, 0, "tps")
+            product(5)
             out0(0, 1, S)
-            interleave(m_tok[1], m_raw[1], 0, 256, S)
-            interleave(da_tok[1], da[1], 0, 256, V)
-            spread_da(3, S)
-            interleave(m_tok[1], m_raw[1], 256, 256, V)
+            mx0(0, 0)
+            spread_da(1, S)
+            diff_tensor(3)
+            load(z, zv, 6, 2)
+            gate(3)
+            finish(2)
+            load_m(0, 0)
+            interleave(m_tok[0], m_raw[0], 0, 256, V)
+            load_mfull(1)
+            out0(0, 0, S)
             store0_slot(1)
-            q_feat(3)
-            out0(5, 1, S)
-            mx0(5, 0)
-            mx0(4, 0)
-            q_tok(1, 0, 512)
-            mx0(4, 1)
-            interleave(m_tok[0], m_raw[0], 512, 256, V)
-            out0(5, 0, S)
-            out0(4, 0, S)
-            out0(4, 1, S)
-            mx0(7, 0)
-            mx1(1, 0, "dps")
-            mx0(7, 1)
+            turn_da(2)
+            interleave(m_tok[0], m_raw[0], 256, 256, S)
+            q_feat(1)
+            mx0(2, 0)
             store0_slot(0)
+            mx0(2, 1)
+            load_m(0, 1)
+            spread_da(2, S)
+            product(7)
+            q_tok(0, 0, 512)
+            product(6)
+            mx0(3, 1)
+            q_feat(2)
+            finish(3)
+            mx0(5, 0)
+            out0(2, 0, S)
+            q_msg(0, 0, 512)
+            out0(2, 1, S)
+            interleave(da_tok[1], da[1], 0, 256, V)
+            store0_slot(2)
+            mx0(5, 1)
+            mx0(3, 0)
+            interleave(m_tok[1], m_raw[1], 256, 256, V)
+            turn_da(3)
+            out0(3, 1, S)
+            out0(5, 0, S)
+            out0(5, 1, S)
+            interleave(m_tok[1], m_raw[1], 0, 256, S)
+            mx0(4, 1)
+            mx0(4, 0)
+            interleave(m_tok[0], m_raw[0], 512, 256, V)
             q_msg(1, 0, 512)
-            mx0(6, 1)
-            mx0(6, 0)
-            mx1(2, 1)
-            interleave(m_tok[0], m_raw[0], 768, 256, V)
             mx1(3, 0, "tps")
-            out0(7, 0, S)
-            out0(7, 1, S)
-            load_m(1, 1)
-            out0(6, 1, S)
-            store0_slot(5)
             mx1(0, 0, "dps")
-            interleave(m_tok[1], m_raw[1], 768, 256, V)
+            spread_da(3, S)
+            mx1(2, 0, "tps")
+            q_feat(3)
+            store0_slot(5)
+            interleave(da_tok[1], da[1], 256, 256, V)
+            out0(3, 0, S)
+            mx0(6, 1)
+            interleave(m_tok[0], m_raw[0], 768, 256, V)
+            q_tok(1, 0, 512)
+            mx0(6, 0)
+            out0(4, 1, S)
+            out0(4, 0, S)
+            out0(6, 1, S)
+            mx0(7, 1)
+            store0_slot(3)
             out0(6, 0, S)
-            store0_slot(4)
-            mx1(3, 1)
             interleave(m_tok[1], m_raw[1], 512, 256, V)
+            interleave(m_tok[1], m_raw[1], 768, 256, V)
+            store0_slot(4)
+            mx1(1, 0, "dps")
+            out0(7, 1, S)
+            store0_slot(6)
             q_msg(0, 512, 512)
+            mx0(7, 0)
+            out0(7, 0, S)
             q_msg(1, 512, 512)
-            mx1(0, 1)
+            mx1(3, 1)
+            mx1(2, 1)
             mx1(1, 1)
+            mx1(0, 1)
             mx1(5, 0, "mps")
             mx1(4, 0, "mps")
             mx1(5, 1)
-            out1(2, S)
             mx1(4, 1)
             mx1(7, 0, "mps")
-            out1(3, S)
-            out1(0, S)
             store0_slot(7)
-            out1(4, V)
             mx1(7, 1)
             mx1(6, 0, "mps")
-            out1(1, S)
-            out1(7, V)
-            out1(5, S)
-            store0_slot(6)
+            out1(5, V)
+            out1(3, S)
+            out1(2, S)
+            out1(0, S)
             mx1(6, 1)
-            out1(6, V)
             store1(2, 2)
+            out1(1, S)
             store1(0, 2)
+            out1(4, S)
+            out1(7, S)
             store1(4, 2)
-            store1(6, 2)
+            store1(7, 1)
+            out1(6, S)
+            store1(6, 1)

@@ -115,7 +115,7 @@ def tile_updatefunction_pb_v_kernel(
                 diffs[2 * c + e] = diff[:, e, :]
 
         def diff_tensor(c):
-            banks2 = [psum.tile([P, FEATS], F32, name="dps") for e in range(2)]
+            banks2 = [psum.tile([P, FEATS], F32, name="aux", bufs=4) for e in range(2)]
             for e in range(2):
                 nc.tensor.matmul(banks2[e][:], lhsT=plus[:], rhs=slot(h, 2 * c + e), start=True, stop=False)
             for e in range(2):
@@ -133,7 +133,7 @@ def tile_updatefunction_pb_v_kernel(
             nc.vector.tensor_mul(out=pair(da, c), in0=prods[c][:], in1=gates[c][:])
 
         def turn_da(c):
-            bank = psum.tile([P, 2, 2, P], F32, name="tps")
+            bank = psum.tile([P, 2, 2, P], F32, name="aux", bufs=4)
             for e in range(2):
                 words = da[c // 2][:, 2 * (c % 2) + e, :].bitcast(F32)
                 for u in range(2):
@@ -147,7 +147,7 @@ def tile_updatefunction_pb_v_kernel(
             )
 
         def turn_w(i, q):
-            bank = psum.tile([P, 2, 2, P], F32, name="tps")
+            bank = psum.tile([P, 2, 2, P], F32, name="aux", bufs=4)
             for r in range(2):
                 words = w_raw[i][:, 2 * q + r, :].bitcast(F32)
                 for u in range(2):
@@ -206,7 +206,7 @@ def tile_updatefunction_pb_v_kernel(
 
         def mx1(m, k, where=None):
             if k == 0:
-                banks["o1", m] = psum.tile([P, 512], F32, name=where, bufs=4 if where == "mps" else 2)
+                banks["o1", m] = psum.tile([P, 512], F32, name=where, bufs=4)
             cols = slice(P * m, P * m + P)
             nc.tensor.matmul_mx(
                 out=banks["o1", m][:], lhsT=q_m[k][0][:, cols].bitcast(E4M3), lhsT_scale=q_m[k][1][:, cols],
@@ -232,149 +232,155 @@ def tile_updatefunction_pb_v_kernel(
         with tc.manual_schedule():
             load(t, tv, 0, 2)
             load(h, hv, 0, 2)
-            diff_vector(0)
             load(z, zv, 0, 2)
+            load(g, gv, 0, 2)
+            load_mask()
+            diff_vector(0)
             gate(0)
             load_w(0)
-            load_mask()
-            turn_w(0, 0)
-            load(g, gv, 0, 2)
-            load(h, hv, 2, 2)
-            product(1)
             product(0)
             turn_w(0, 1)
-            finish(0)
-            load(t, tv, 2, 2)
-            diff_tensor(1)
-            load(z, zv, 2, 2)
-            load_w(1)
             spread_w(0, 1, S)
+            load(h, hv, 2, 2)
+            turn_w(0, 0)
+            product(1)
+            finish(0)
+            load(z, zv, 2, 2)
+            load(t, tv, 2, 2)
             gate(1)
-            load(g, gv, 2, 2)
-            spread_w(0, 0, S)
+            diff_tensor(1)
             turn_da(0)
-            q_weight(0)
-            spread_da(0, S)
+            spread_w(0, 0, S)
+            load(g, gv, 2, 2)
+            load_w(1)
             load(z, zv, 4, 2)
+            q_weight(0)
             product(2)
-            product(3)
-            turn_w(1, 0)
-            spread_w(1, 0, S)
+            spread_da(0, S)
+            load(t, tv, 4, 2)
+            load(h, hv, 4, 2)
+            load(g, gv, 4, 2)
             turn_w(1, 1)
+            turn_w(1, 0)
+            load(h, hv, 6, 2)
             spread_w(1, 1, S)
-            load(h, hv, 4, 4)
+            product(3)
+            spread_w(1, 0, S)
             q_feat(0)
-            mx0(1, 0)
-            out0(1, 0, S)
-            finish(1)
-            interleave(da_tok[0], da[0], 256, 256, S)
-            gate(2)
-            load(t, tv, 4, 4)
-            q_weight(1)
-            interleave(da_tok[0], da[0], 0, 256, S)
-            diff_tensor(2)
-            turn_da(1)
-            mx0(1, 1)
-            out0(1, 1, S)
-            load(g, gv, 4, 4)
-            product(4)
-            mx0(0, 1)
-            product(5)
-            out0(0, 1, S)
-            mx0(0, 0)
-            spread_da(1, S)
-            diff_tensor(3)
             load(z, zv, 6, 2)
-            gate(3)
-            finish(2)
+            finish(1)
             load_m(0, 0)
+            gate(2)
+            q_weight(1)
+            mx0(1, 0)
+            diff_tensor(2)
+            product(4)
+            product(5)
+            out0(1, 0, S)
+            interleave(da_tok[0], da[0], 256, 256, S)
+            gate(3)
+            turn_da(1)
+            interleave(da_tok[0], da[0], 0, 256, S)
+            mx0(1, 1)
+            mx0(0, 0)
+            finish(2)
+            mx0(0, 1)
+            load(t, tv, 6, 2)
             interleave(m_tok[0], m_raw[0], 0, 256, V)
-            load_mfull(1)
-            out0(0, 0, S)
-            store0_slot(1)
+            diff_tensor(3)
+            load(g, gv, 6, 2)
             turn_da(2)
-            interleave(m_tok[0], m_raw[0], 256, 256, S)
+            spread_da(1, S)
+            out0(1, 1, S)
+            out0(0, 0, S)
             q_feat(1)
-            mx0(2, 0)
-            store0_slot(0)
-            mx0(2, 1)
-            load_m(0, 1)
-            spread_da(2, S)
-            product(7)
-            q_tok(0, 0, 512)
-            product(6)
-            mx0(3, 1)
-            q_feat(2)
-            finish(3)
-            mx0(5, 0)
-            out0(2, 0, S)
-            q_msg(0, 0, 512)
-            out0(2, 1, S)
-            interleave(da_tok[1], da[1], 0, 256, V)
-            store0_slot(2)
-            mx0(5, 1)
             mx0(3, 0)
-            interleave(m_tok[1], m_raw[1], 256, 256, V)
-            turn_da(3)
-            out0(3, 1, S)
-            out0(5, 0, S)
-            out0(5, 1, S)
-            interleave(m_tok[1], m_raw[1], 0, 256, S)
-            mx0(4, 1)
-            mx0(4, 0)
-            interleave(m_tok[0], m_raw[0], 512, 256, V)
-            q_msg(1, 0, 512)
-            mx1(3, 0, "tps")
-            mx1(0, 0, "dps")
-            spread_da(3, S)
-            mx1(2, 0, "tps")
-            q_feat(3)
-            store0_slot(5)
-            interleave(da_tok[1], da[1], 256, 256, V)
+            out0(0, 1, S)
+            product(6)
+            interleave(m_tok[0], m_raw[0], 256, 256, S)
+            spread_da(2, S)
+            q_tok(0, 0, 512)
+            product(7)
+            mx0(2, 1)
             out0(3, 0, S)
-            mx0(6, 1)
-            interleave(m_tok[0], m_raw[0], 768, 256, V)
-            q_tok(1, 0, 512)
-            mx0(6, 0)
-            out0(4, 1, S)
+            q_feat(2)
+            mx0(2, 0)
+            finish(3)
+            out0(2, 1, S)
+            q_msg(0, 0, 512)
+            load_mfull(1)
+            out0(2, 0, S)
+            store0_slot(1)
+            store0_slot(0)
+            mx0(3, 1)
+            out0(3, 1, S)
+            mx0(4, 0)
+            load_m(0, 1)
+            store0_slot(2)
+            mx0(4, 1)
+            turn_da(3)
+            interleave(da_tok[1], da[1], 256, 256, V)
+            interleave(m_tok[1], m_raw[1], 0, 256, S)
+            interleave(da_tok[1], da[1], 0, 256, V)
+            spread_da(3, S)
             out0(4, 0, S)
+            interleave(m_tok[0], m_raw[0], 768, 256, V)
+            out0(4, 1, S)
+            q_feat(3)
+            interleave(m_tok[1], m_raw[1], 256, 256, V)
+            q_tok(1, 0, 512)
+            interleave(m_tok[0], m_raw[0], 512, 256, V)
+            mx1(1, 0, "aux")
+            store0_slot(3)
+            mx0(5, 0)
+            out0(5, 0, S)
+            mx0(5, 1)
+            mx1(0, 0, "aux")
+            store0_slot(4)
+            mx1(2, 0, "aux")
+            mx0(6, 1)
+            mx0(6, 0)
+            mx0(7, 0)
+            out0(5, 1, S)
             out0(6, 1, S)
             mx0(7, 1)
-            store0_slot(3)
+            mx1(3, 0, "aux")
             out0(6, 0, S)
-            interleave(m_tok[1], m_raw[1], 512, 256, V)
-            interleave(m_tok[1], m_raw[1], 768, 256, V)
-            store0_slot(4)
-            mx1(1, 0, "dps")
-            out0(7, 1, S)
-            store0_slot(6)
-            q_msg(0, 512, 512)
-            mx0(7, 0)
-            out0(7, 0, S)
-            q_msg(1, 512, 512)
+            q_msg(1, 0, 512)
             mx1(3, 1)
             mx1(2, 1)
-            mx1(1, 1)
+            store0_slot(5)
+            store0_slot(6)
+            interleave(m_tok[1], m_raw[1], 512, 256, V)
+            out0(7, 1, S)
+            q_msg(0, 512, 512)
+            out0(7, 0, S)
             mx1(0, 1)
-            mx1(5, 0, "mps")
-            mx1(4, 0, "mps")
-            mx1(5, 1)
-            mx1(4, 1)
+            mx1(1, 1)
             mx1(7, 0, "mps")
-            store0_slot(7)
-            mx1(7, 1)
-            mx1(6, 0, "mps")
-            out1(5, V)
+            mx1(4, 0, "mps")
+            interleave(m_tok[1], m_raw[1], 768, 256, V)
             out1(3, S)
-            out1(2, S)
-            out1(0, S)
+            q_msg(1, 512, 512)
+            mx1(6, 0, "mps")
+            store0_slot(7)
             mx1(6, 1)
-            store1(2, 2)
+            out1(0, V)
+            mx1(7, 1)
+            store1(3, 1)
+            out1(2, S)
+            store1(2, 1)
             out1(1, S)
-            store1(0, 2)
-            out1(4, S)
-            out1(7, S)
-            store1(4, 2)
-            store1(7, 1)
-            out1(6, S)
+            store1(1, 1)
+            store1(0, 1)
+            mx1(4, 1)
+            out1(6, V)
+            out1(7, V)
+            mx1(5, 0, "mps")
+            out1(4, V)
+            mx1(5, 1)
             store1(6, 1)
+            out1(5, V)
+            store1(7, 1)
+            store1(4, 1)
+            store1(5, 1)

from contextlib import ExitStack

import concourse.mybir as mybir
from concourse.masks import make_identity

TOKENS, FEATS, MSG = 1024, 512, 1024
FLOPS = 2 * 2 * TOKENS * FEATS * MSG
BYTES = 2 * TOKENS * (3 * FEATS + MSG + 1) + 2 * MSG * FEATS + 4 * TOKENS * FEATS + 4 * (TOKENS * MSG + MSG * FEATS)

F32 = mybir.dt.float32
BF16 = mybir.dt.bfloat16
U32 = mybir.dt.uint32
U8 = mybir.dt.uint8
E4M3 = mybir.dt.float8_e4m3fn_x4
E5M2 = mybir.dt.float8_e5m2_x4
ADD = mybir.AluOpType.add
MULT = mybir.AluOpType.mult

P = 128
PASSES = 2
SLOTS = 4
PAIRS = 4


def tile_updatefunction_pb_v_kernel(
    tc, node_state, message, h_tilda, mask, w_z, u_z, z_t, grad_out, out_0, out_1
):
    nc = tc.nc
    by_slot = "(g p j) w -> g p j w"
    hv = node_state.rearrange("b n w -> (b n) w").rearrange(by_slot, g=PASSES, j=SLOTS)
    tv = h_tilda.rearrange(by_slot, g=PASSES, j=SLOTS)
    zv = z_t.rearrange(by_slot, g=PASSES, j=SLOTS)
    gv = grad_out.rearrange("b n w -> (b n) w").rearrange(by_slot, g=PASSES, j=SLOTS)
    mv = message.rearrange("b n w -> (b n) w").rearrange(by_slot, g=PASSES, j=SLOTS)
    kv = mask.rearrange("b n -> (b n)").rearrange("(g p j) -> p g j", g=PASSES, j=SLOTS)
    wv = w_z.rearrange("(i p r) d -> i p r d", i=2, r=4)
    o0v = out_0.rearrange("b n w -> (b n) w").rearrange(by_slot, g=PASSES, j=SLOTS)
    o1v = out_1.rearrange("(m p) d -> p m d", p=P)

    with ExitStack() as ctx:
        keep = ctx.enter_context(tc.tile_pool(name="keep", bufs=1))
        work = ctx.enter_context(tc.tile_pool(name="work", bufs=3))
        psum = ctx.enter_context(tc.psum_pool(name="psum", bufs=2))

        def kept(name, shape, dtype):
            return keep.tile(shape, dtype, name=name, align_bytes=64)

        ident = kept("ident", [P, P], F32)
        plus = kept("plus", [P, P], BF16)
        minus = kept("minus", [P, P], BF16)
        mk = kept("mk", [P, PASSES, SLOTS], BF16)
        z = [kept(f"z{k}", [P, SLOTS, FEATS], F32) for k in range(PASSES)]
        h = [kept(f"h{k}", [P, SLOTS, FEATS], BF16) for k in range(PASSES)]
        t = [kept(f"t{k}", [P, SLOTS, FEATS], BF16) for k in range(PASSES)]
        g = [kept(f"g{k}", [P, SLOTS, FEATS], BF16) for k in range(PASSES)]
        w_raw = [kept(f"w_raw{i}", [P, 4, FEATS], BF16) for i in range(2)]
        m_raw = [kept(f"m_raw{k}", [P, SLOTS, MSG], BF16) for k in range(PASSES)]

        da = [kept(f"da{k}", [P, SLOTS, FEATS], BF16) for k in range(PASSES)]
        da_tok = [kept(f"da_tok{k}", [P, FEATS, 4], BF16) for k in range(PASSES)]
        da_feat = [kept(f"da_feat{c}", [P, 2 * P * 4], BF16) for c in range(PAIRS)]
        m_tok = [kept(f"m_tok{k}", [P, MSG, 4], BF16) for k in range(PASSES)]
        w_feat = [kept(f"w_feat{i}", [P, 512 * 4], BF16) for i in range(2)]

        def quantised(name, width):
            return kept(name + "_codes", [P, width], U32), kept(name + "_scales", [P, width], U8)

        q_da_tok = [quantised(f"q_da_tok{k}", FEATS) for k in range(PASSES)]
        q_da_feat = [quantised(f"q_da_feat{c}", 2 * P) for c in range(PAIRS)]
        q_m = [quantised(f"q_m{k}", MSG) for k in range(PASSES)]
        q_w = [quantised(f"q_w{i}", 512) for i in range(2)]

        o0 = [kept(f"o0_{c}", [P, 2, MSG], F32) for c in range(PAIRS)]
        o1 = kept("o1", [P, 8, FEATS], F32)

        def span(first, count):
            return first // SLOTS, slice(first % SLOTS, first % SLOTS + count)

        def load(dst, view, first, count):
            k, slots = span(first, count)
            nc.sync.dma_start(out=dst[k][:, slots, :], in_=view[k][:, slots, :])

        def load_m(k, half):
            cols = slice(512 * half, 512 * half + 512)
            nc.sync.dma_start(out=m_raw[k][:, :, cols], in_=mv[k][:, :, cols])

        def load_mfull(k):
            nc.sync.dma_start(out=m_raw[k][:], in_=mv[k])

        def load_mask():
            nc.sync.dma_start(out=mk[:], in_=kv)

        def load_w(i):
            nc.sync.dma_start(out=w_raw[i][:], in_=wv[i])

        def slot(tiles, s):
            return tiles[s // SLOTS][:, s % SLOTS, :]

        def pair(tiles, c):
            return tiles[c // 2][:, 2 * (c % 2) : 2 * (c % 2) + 2, :]

        gates = {}
        diffs = {}
        prods = {}

        def gate(c):
            gates[c] = work.tile([P, 2, FEATS], F32, name="gate")
            prods[c] = work.tile([P, 2, FEATS], F32, name="prod")
            nc.vector.scalar_tensor_tensor(out=gates[c][:], in0=pair(z, c), scalar=-1.0, in1=pair(z, c), op0=ADD, op1=MULT)

        def diff_vector(c):
            diff = work.tile([P, 2, FEATS], F32, name="diff", bufs=1)
            nc.vector.tensor_sub(out=diff[:], in0=pair(h, c), in1=pair(t, c))
            for e in range(2):
                diffs[2 * c + e] = diff[:, e, :]

        def diff_tensor(c):
            banks2 = [psum.tile([P, FEATS], F32, name="aux", bufs=4) for e in range(2)]
            for e in range(2):
                nc.tensor.matmul(banks2[e][:], lhsT=plus[:], rhs=slot(h, 2 * c + e), start=True, stop=False)
            for e in range(2):
                nc.tensor.matmul(banks2[e][:], lhsT=minus[:], rhs=slot(t, 2 * c + e), start=False, stop=True)
                diffs[2 * c + e] = banks2[e][:]

        def product(s):
            c, e = s // 2, s % 2
            nc.vector.scalar_tensor_tensor(
                out=prods[c][:, e, :], in0=slot(g, s), scalar=mk[:, s // SLOTS, s % SLOTS : s % SLOTS + 1],
                in1=diffs[s], op0=MULT, op1=MULT,
            )

        def finish(c):
            nc.vector.tensor_mul(out=pair(da, c), in0=prods[c][:], in1=gates[c][:])

        def turn_da(c):
            bank = psum.tile([P, 2, 2, P], F32, name="aux", bufs=4)
            for e in range(2):
                words = da[c // 2][:, 2 * (c % 2) + e, :].bitcast(F32)
                for u in range(2):
                    nc.tensor.transpose(bank[:, e, u, :], words[:, u : FEATS // 2 : 2], ident[:])
            diffs["da", c] = bank

        def spread_da(c, copy):
            copy(
                out=da_feat[c][:].bitcast(F32).rearrange("p (e k u) -> p e k u", e=2, u=2),
                in_=diffs["da", c][:].rearrange("p e u k -> p e k u"),
            )

        def turn_w(i, q):
            bank = psum.tile([P, 2, 2, P], F32, name="aux", bufs=4)
            for r in range(2):
                words = w_raw[i][:, 2 * q + r, :].bitcast(F32)
                for u in range(2):
                    nc.tensor.transpose(bank[:, r, u, :], words[:, u : FEATS // 2 : 2], ident[:])
            diffs["w", i, q] = bank

        def spread_w(i, q, copy):
            words = w_feat[i][:].bitcast(F32).rearrange("p (k r u) -> p k r u", r=4, u=2)
            copy(out=words[:, :, 2 * q : 2 * q + 2, :], in_=diffs["w", i, q][:].rearrange("p r u k -> p k r u"))

        def interleave(dst, src, first, width, copy):
            cols = slice(first, first + width)
            copy(
                out=dst[:, cols, :].rearrange("p (c i) t -> p c t i", i=4),
                in_=src[:, :, cols].rearrange("p t (c i) -> p c t i", i=4),
            )

        def quantise(dst, src, first, width, fmt):
            codes, scales = dst
            nc.vector.quantize_mx(
                out=codes[:, first : first + width].bitcast(fmt), scales=scales[:, first : first + width], in_=src
            )

        def q_tok(k, first, width):
            quantise(q_da_tok[k], da_tok[k][:, first : first + width, :].rearrange("p w t -> p (w t)"), first, width, E5M2)

        def q_feat(c):
            quantise(q_da_feat[c], da_feat[c][:], 0, 2 * P, E5M2)

        def q_msg(k, first, width):
            quantise(q_m[k], m_tok[k][:, first : first + width, :].rearrange("p w t -> p (w t)"), first, width, E4M3)

        def q_weight(i):
            quantise(q_w[i], w_feat[i][:], 0, 512, E4M3)

        banks = {}

        def mx0(s, n):
            c, e = s // 2, s % 2
            bank = psum.tile([P, 512], F32, name="mps", bufs=4)
            cols = slice(P * e, P * e + P)
            nc.tensor.matmul_mx(
                out=bank[:], lhsT=q_da_feat[c][0][:, cols].bitcast(E5M2), lhsT_scale=q_da_feat[c][1][:, cols],
                rhs=q_w[n][0][:].bitcast(E4M3), rhs_scale=q_w[n][1][:], start=True, stop=True,
            )
            banks[s, n] = bank

        def out0(s, n, copy):
            copy(out=o0[s // 2][:, s % 2, 512 * n : 512 * n + 512], in_=banks[s, n][:])

        def store0(c):
            nc.sync.dma_start(out=o0v[c // 2][:, 2 * (c % 2) : 2 * (c % 2) + 2, :], in_=o0[c][:])

        def store0_slot(s):
            nc.sync.dma_start(out=o0v[s // 4][:, s % 4, :], in_=o0[s // 2][:, s % 2, :])

        def mx1(m, k, where=None):
            if k == 0:
                banks["o1", m] = psum.tile([P, 512], F32, name=where, bufs=4)
            cols = slice(P * m, P * m + P)
            nc.tensor.matmul_mx(
                out=banks["o1", m][:], lhsT=q_m[k][0][:, cols].bitcast(E4M3), lhsT_scale=q_m[k][1][:, cols],
                rhs=q_da_tok[k][0][:].bitcast(E5M2), rhs_scale=q_da_tok[k][1][:], start=(k == 0), stop=(k == 1),
            )

        def out1(m, copy):
            copy(out=o1[:, m, :], in_=banks["o1", m][:])

        def store1(m, count):
            nc.sync.dma_start(out=o1v[:, m : m + count, :], in_=o1[:, m : m + count, :])

        V, S = nc.vector.tensor_copy, nc.scalar.copy

        make_identity(nc, plus[:])
        nc.gpsimd.memset(minus[:], 0.0)
        nc.gpsimd.affine_select(
            out=minus[:], in_=minus[:], compare_op=mybir.AluOpType.not_equal, fill=-1.0, base=0,
            pattern=[[-1, P]], channel_multiplier=1,
        )
        make_identity(nc, ident[:])

        with tc.manual_schedule():
            load(t, tv, 0, 2)
            load(h, hv, 0, 2)
            load(z, zv, 0, 2)
            load(g, gv, 0, 2)
            load_mask()
            diff_vector(0)
            gate(0)
            load_w(0)
            product(0)
            turn_w(0, 1)
            spread_w(0, 1, S)
            load(h, hv, 2, 2)
            turn_w(0, 0)
            product(1)
            finish(0)
            load(z, zv, 2, 2)
            load(t, tv, 2, 2)
            gate(1)
            diff_tensor(1)
            turn_da(0)
            spread_w(0, 0, S)
            load(g, gv, 2, 2)
            load_w(1)
            load(z, zv, 4, 2)
            q_weight(0)
            product(2)
            spread_da(0, S)
            load(t, tv, 4, 2)
            load(h, hv, 4, 2)
            load(g, gv, 4, 2)
            turn_w(1, 1)
            turn_w(1, 0)
            load(h, hv, 6, 2)
            spread_w(1, 1, S)
            product(3)
            spread_w(1, 0, S)
            q_feat(0)
            load(z, zv, 6, 2)
            finish(1)
            load_m(0, 0)
            gate(2)
            q_weight(1)
            mx0(1, 0)
            diff_tensor(2)
            product(4)
            product(5)
            out0(1, 0, S)
            interleave(da_tok[0], da[0], 256, 256, S)
            gate(3)
            turn_da(1)
            interleave(da_tok[0], da[0], 0, 256, S)
            mx0(1, 1)
            mx0(0, 0)
            finish(2)
            mx0(0, 1)
            load(t, tv, 6, 2)
            interleave(m_tok[0], m_raw[0], 0, 256, V)
            diff_tensor(3)
            load(g, gv, 6, 2)
            turn_da(2)
            spread_da(1, S)
            out0(1, 1, S)
            out0(0, 0, S)
            q_feat(1)
            mx0(3, 0)
            out0(0, 1, S)
            product(6)
            interleave(m_tok[0], m_raw[0], 256, 256, S)
            spread_da(2, S)
            q_tok(0, 0, 512)
            product(7)
            mx0(2, 1)
            out0(3, 0, S)
            q_feat(2)
            mx0(2, 0)
            finish(3)
            out0(2, 1, S)
            q_msg(0, 0, 512)
            load_mfull(1)
            out0(2, 0, S)
            store0_slot(1)
            store0_slot(0)
            mx0(3, 1)
            out0(3, 1, S)
            mx0(4, 0)
            load_m(0, 1)
            store0_slot(2)
            mx0(4, 1)
            turn_da(3)
            interleave(da_tok[1], da[1], 256, 256, V)
            interleave(m_tok[1], m_raw[1], 0, 256, S)
            interleave(da_tok[1], da[1], 0, 256, V)
            spread_da(3, S)
            out0(4, 0, S)
            interleave(m_tok[0], m_raw[0], 768, 256, V)
            out0(4, 1, S)
            q_feat(3)
            interleave(m_tok[1], m_raw[1], 256, 256, V)
            q_tok(1, 0, 512)
            interleave(m_tok[0], m_raw[0], 512, 256, V)
            mx1(1, 0, "aux")
            store0_slot(3)
            mx0(5, 0)
            out0(5, 0, S)
            mx0(5, 1)
            mx1(0, 0, "aux")
            store0_slot(4)
            mx1(2, 0, "aux")
            mx0(6, 1)
            mx0(6, 0)
            mx0(7, 0)
            out0(5, 1, S)
            out0(6, 1, S)
            mx0(7, 1)
            mx1(3, 0, "aux")
            out0(6, 0, S)
            q_msg(1, 0, 512)
            mx1(3, 1)
            mx1(2, 1)
            store0_slot(5)
            store0_slot(6)
            interleave(m_tok[1], m_raw[1], 512, 256, V)
            out0(7, 1, S)
            q_msg(0, 512, 512)
            out0(7, 0, S)
            mx1(0, 1)
            mx1(1, 1)
            mx1(7, 0, "mps")
            mx1(4, 0, "mps")
            interleave(m_tok[1], m_raw[1], 768, 256, V)
            out1(3, S)
            q_msg(1, 512, 512)
            mx1(6, 0, "mps")
            store0_slot(7)
            mx1(6, 1)
            out1(0, V)
            mx1(7, 1)
            store1(3, 1)
            out1(2, S)
            store1(2, 1)
            out1(1, S)
            store1(1, 1)
            store1(0, 1)
            mx1(4, 1)
            out1(6, V)
            out1(7, V)
            mx1(5, 0, "mps")
            out1(4, V)
            mx1(5, 1)
            store1(6, 1)
            out1(5, V)
            store1(7, 1)
            store1(4, 1)
            store1(5, 1)
